import numpy as np
import ml_dtypes


def mxq(x, axis, fmt="e4m3"):
    dtype, down = {"e4m3": (ml_dtypes.float8_e4m3fn, 7), "e5m2": (ml_dtypes.float8_e5m2, 14)}[fmt]
    v = np.moveaxis(np.asarray(x, np.float32).astype(ml_dtypes.bfloat16).astype(np.float64), axis, -1)
    blocks = v.reshape(v.shape[:-1] + (-1, 32))
    amax = np.abs(blocks).max(-1, keepdims=True)
    byte = np.maximum(np.where(amax > 0, np.frexp(amax)[1] - 1 + 127, 0) - down, 1)
    scale = np.exp2(byte - 127.0)
    codes = (blocks / scale).astype(np.float32).astype(dtype).astype(np.float64)
    return np.moveaxis((codes * scale).reshape(v.shape), -1, axis)


WIDE = False


def mx_kscale(k):
    if not WIDE:
        return np.ones(k)
    levels = np.array([10, -10, 5, -5, 0])
    a = np.random.permutation(np.resize(levels, k // 512 * 4)).reshape(k // 512, 4)
    idx = np.arange(k)
    return np.exp2(a[idx // 512, idx % 128 // 32])


BF16 = ml_dtypes.bfloat16


def bf(x):
    return np.asarray(x, np.float32).astype(BF16)


def f64(x):
    return np.asarray(x).astype(np.float64)


B, N, D, H, S = 2, 512, 512, 1024, 128
QS = 2.3 / N ** 0.25


def silu(z):
    return z / (1.0 + np.exp(-z))


def setup_inputs():
    t = np.exp2(np.round(np.log2(mx_kscale(N)) / 2))
    r = mx_kscale(H)
    return {"q": bf(np.random.standard_normal((B, N, S)) * QS),
            "k": bf(np.random.standard_normal((B, N, S)) * QS * t[:, None]),
            "u": bf(silu(0.7 * np.random.standard_normal((B, N, H))) * r),
            "v": bf(silu(0.7 * np.random.standard_normal((B, N, H))) / (t * t)[:, None]),
            "W_o": bf(np.random.standard_normal((H, D)) / np.sqrt(H) / r[:, None]),
            "b_o": bf(0.1 * np.random.standard_normal(D))}


def reference(q, k, u, v, W_o, b_o):
    qk = f64(q) @ f64(k).transpose(0, 2, 1) * (1.0 / np.sqrt(S))
    attn = np.square(np.maximum(qk, 0.0))
    av = mxq(attn, 2, "e4m3") @ mxq(f64(v), 1, "e4m3")
    gated = f64(u) * av
    return (mxq(gated, 2, "e4m3") @ mxq(f64(W_o), 0, "e4m3")) + f64(b_o)

@@ -1,0 +1,227 @@
+import math
+from contextlib import ExitStack
+
+import concourse.mybir as mybir
+from concourse.masks import make_identity
+
+BF16 = mybir.dt.bfloat16
+F32 = mybir.dt.float32
+U32 = mybir.dt.uint32
+U8 = mybir.dt.uint8
+FP8X4 = mybir.dt.float8_e4m3fn_x4
+ACT = mybir.ActivationFunctionType
+ALU = mybir.AluOpType
+
+P = 128
+PACK = 4
+B, N, S, H, D = 2, 512, 128, 1024, 512
+CHUNKS = N // P
+PASSES = H // (P * PACK)
+
+FLOPS = 2 * B * N * N * S + 2 * B * N * N * H + 2 * B * N * H * D
+
+
+def regroup(copy, grouped, rows):
+    copy(
+        out=grouped.rearrange("p (c i) t -> p c t i", i=4),
+        in_=rows.rearrange("p t (c i) -> p c t i", i=4),
+    )
+
+
+def quantise(nc, grouped, codes, scales):
+    nc.vector.quantize_mx(out=codes.bitcast(FP8X4), scales=scales, in_=grouped)
+
+
+def tile_gatedattentionunit_pb_kernel(tc, q, k, u, v, W_o, b_o, out):
+    nc = tc.nc
+    halves = [slice(g * (H // 2), (g + 1) * (H // 2)) for g in range(PASSES)]
+    with ExitStack() as ctx:
+        const = ctx.enter_context(tc.tile_pool(name="const", bufs=1))
+        batch = ctx.enter_context(tc.tile_pool(name="batch", bufs=B))
+        work = ctx.enter_context(tc.tile_pool(name="work", bufs=2))
+        psum = ctx.enter_context(tc.psum_pool(name="psum", bufs=4))
+
+        identity = const.tile([P, P], BF16)
+        make_identity(nc, identity[:])
+
+        k_rows, q_rows, v_rows, u_rows = [], [], [], []
+        k_flipped, q_flipped, u_flipped = [], [], []
+        attn_mx, v_mx, gated_mx = [], [], []
+        for b in range(B):
+            k_sb = batch.tile([P, PACK, S], BF16)
+            q_sb = batch.tile([P, CHUNKS, S], BF16)
+            v_sb = batch.tile([P, PACK, H], BF16)
+            u_sb = batch.tile([P, CHUNKS, H], BF16)
+            kT = batch.tile([P, PACK, P], BF16)
+            qT = batch.tile([P, CHUNKS, P], BF16)
+            uT = batch.tile([P, PASSES, CHUNKS, PACK, P], BF16)
+            attn_grouped = batch.tile([P, CHUNKS, P, PACK], BF16, align_bytes=64)
+            attn_codes = batch.tile([P, N], U32, align_bytes=64)
+            attn_scales = batch.tile([P, N], U8, align_bytes=64)
+            v_grouped = batch.tile([P, H, PACK], BF16, align_bytes=64)
+            v_codes = batch.tile([P, H], U32, align_bytes=64)
+            v_scales = batch.tile([P, H], U8, align_bytes=64)
+            gated_grouped = batch.tile([P, PASSES, CHUNKS, P, PACK], BF16, align_bytes=64)
+            gated_codes = batch.tile([P, PASSES, N], U32, align_bytes=64)
+            gated_scales = batch.tile([P, PASSES, N], U8, align_bytes=64)
+            k_rows.append(k_sb)
+            q_rows.append(q_sb)
+            v_rows.append(v_sb)
+            u_rows.append(u_sb)
+            k_flipped.append(kT)
+            q_flipped.append(qT)
+            u_flipped.append(uT)
+            attn_mx.append((attn_grouped, attn_codes, attn_scales))
+            v_mx.append((v_grouped, v_codes, v_scales))
+            gated_mx.append((gated_grouped, gated_codes, gated_scales))
+        w_sb = const.tile([P, PASSES, PACK, D], BF16)
+        w_grouped = const.tile([P, PASSES, D, PACK], BF16, align_bytes=64)
+        w_codes = const.tile([P, PASSES, D], U32, align_bytes=64)
+        w_scales = const.tile([P, PASSES, D], U8, align_bytes=64)
+        bias = const.tile([P, D], BF16)
+
+        def load_small(b):
+            nc.sync.dma_start(out=k_rows[b][:], in_=k[b].rearrange("(p t) s -> p t s", t=PACK))
+            nc.sync.dma_start(out=q_rows[b][:], in_=q[b].rearrange("(p c) s -> p c s", c=CHUNKS))
+
+        def load_wide(rows_sb, rows):
+            for half in halves:
+                nc.sync.dma_start(
+                    out=rows_sb[:, :, half], in_=rows.rearrange("(p i) h -> p i h", i=PACK)[:, :, half]
+                )
+
+        load_small(0)
+        load_wide(v_rows[0], v[0])
+        load_wide(v_rows[1], v[1])
+        load_wide(u_rows[0], u[0])
+        load_small(1)
+        load_wide(u_rows[1], u[1])
+        for g in range(PASSES):
+            nc.sync.dma_start(
+                out=w_sb[:, g], in_=W_o[halves[g], :].rearrange("(t p) d -> p t d", t=PACK)
+            )
+        nc.sync.dma_start(out=bias[:], in_=b_o.partition_broadcast(P))
+
+        def transpose_four(blocks, flipped_sb):
+            flipped = psum.tile([P, PACK, P], BF16, tag="plain")
+            for i in range(PACK):
+                nc.tensor.transpose(flipped[:, i, :], blocks[i], identity[:])
+            nc.scalar.copy(out=flipped_sb, in_=flipped[:])
+
+        def transpose_keys_and_queries(b):
+            transpose_four([k_rows[b][:, t, :] for t in range(PACK)], k_flipped[b][:])
+            transpose_four([q_rows[b][:, c, :] for c in range(CHUNKS)], q_flipped[b][:])
+
+        def attention_weights(b):
+            for c in range(CHUNKS):
+                scores = psum.tile([P, PACK, P], F32, tag="plain")
+                for t in range(PACK):
+                    nc.tensor.matmul(
+                        out=scores[:, t, :],
+                        lhsT=k_flipped[b][:, t, :],
+                        rhs=q_flipped[b][:, c, :],
+                        start=True,
+                        stop=True,
+                    )
+                positive = work.tile([P, P, PACK], F32)
+                nc.scalar.activation(
+                    out=positive[:],
+                    in_=scores[:].rearrange("p t n -> p n t"),
+                    func=ACT.Relu,
+                    scale=1.0 / math.sqrt(S),
+                )
+                nc.scalar.activation(out=attn_mx[b][0][:, c], in_=positive[:], func=ACT.Square)
+
+        def quantise_attention_weights(b):
+            grouped, codes, scales = attn_mx[b]
+            quantise(nc, grouped[:].rearrange("p c n t -> p (c n t)"), codes[:], scales[:])
+
+        def regroup_values(b):
+            for half in halves:
+                regroup(nc.vector.tensor_copy, v_mx[b][0][:, half, :], v_rows[b][:, :, half])
+
+        def quantise_values(b):
+            grouped, codes, scales = v_mx[b]
+            for half in halves:
+                quantise(
+                    nc, grouped[:, half, :].rearrange("p h t -> p (h t)"), codes[:, half], scales[:, half]
+                )
+
+        def transpose_gate(b):
+            for g in range(PASSES):
+                for c in range(CHUNKS):
+                    hidden = [slice((g * PACK + t) * P, (g * PACK + t + 1) * P) for t in range(PACK)]
+                    transpose_four([u_rows[b][:, c, columns] for columns in hidden], u_flipped[b][:, g, c])
+
+        def gated_values(b, g):
+            grouped, codes, scales = gated_mx[b]
+            for c in range(CHUNKS):
+                queries = slice(c * P, (c + 1) * P)
+                av = psum.tile([P, PACK, P], F32, tag="mx")
+                for t in range(PACK):
+                    hidden = slice((g * PACK + t) * P, (g * PACK + t + 1) * P)
+                    nc.tensor.matmul_mx(
+                        out=av[:, t, :],
+                        lhsT=v_mx[b][1][:, hidden].bitcast(FP8X4),
+                        lhsT_scale=v_mx[b][2][:, hidden],
+                        rhs=attn_mx[b][1][:, queries].bitcast(FP8X4),
+                        rhs_scale=attn_mx[b][2][:, queries],
+                        start=True,
+                        stop=True,
+                    )
+                nc.vector.tensor_tensor(
+                    out=grouped[:, g, c],
+                    in0=av[:].rearrange("p t n -> p n t"),
+                    in1=u_flipped[b][:, g, c].rearrange("p t n -> p n t"),
+                    op=ALU.mult,
+                )
+            quantise(nc, grouped[:, g].rearrange("p c n t -> p (c n t)"), codes[:, g, :], scales[:, g, :])
+
+        def regroup_weights():
+            for g in range(PASSES):
+                regroup(nc.scalar.copy, w_grouped[:, g], w_sb[:, g])
+
+        def quantise_weights(g):
+            quantise(nc, w_grouped[:, g].rearrange("p d t -> p (d t)"), w_codes[:, g, :], w_scales[:, g, :])
+
+        def project(b):
+            out_chunks = out[b].rearrange("(p c) d -> p c d", c=CHUNKS)
+            result = batch.tile([P, CHUNKS, D], F32)
+            for c in range(CHUNKS):
+                queries = slice(c * P, (c + 1) * P)
+                acc = psum.tile([P, D], F32, tag="mx")
+                for g in range(PASSES):
+                    nc.tensor.matmul_mx(
+                        out=acc[:],
+                        lhsT=gated_mx[b][1][:, g, queries].bitcast(FP8X4),
+                        lhsT_scale=gated_mx[b][2][:, g, queries],
+                        rhs=w_codes[:, g, :].bitcast(FP8X4),
+                        rhs_scale=w_scales[:, g, :],
+                        start=(g == 0),
+                        stop=(g == PASSES - 1),
+                    )
+                nc.vector.tensor_tensor(out=result[:, c, :], in0=acc[:], in1=bias[:], op=ALU.add)
+                nc.sync.dma_start(out=out_chunks[:, c, :], in_=result[:, c, :])
+
+        with tc.manual_schedule():
+            transpose_keys_and_queries(0)
+            attention_weights(0)
+            regroup_values(0)
+            quantise_values(0)
+            regroup_values(1)
+            quantise_attention_weights(0)
+            quantise_values(1)
+            transpose_gate(0)
+            transpose_keys_and_queries(1)
+            gated_values(0, 0)
+            attention_weights(1)
+            gated_values(0, 1)
+            quantise_attention_weights(1)
+            transpose_gate(1)
+            regroup_weights()
+            gated_values(1, 0)
+            quantise_weights(0)
+            gated_values(1, 1)
+            quantise_weights(1)
+            project(0)
+            project(1)

@@ -14,18 +14,13 @@ ALU = mybir.AluOpType
 
 P = 128
 PACK = 4
+PAIR = 2
 B, N, S, H, D = 2, 512, 128, 1024, 512
 CHUNKS = N // P
 PASSES = H // (P * PACK)
+SPAN = P * PAIR
 
 FLOPS = 2 * B * N * N * S + 2 * B * N * N * H + 2 * B * N * H * D
-
-
-def regroup(copy, grouped, rows):
-    copy(
-        out=grouped.rearrange("p (c i) t -> p c t i", i=4),
-        in_=rows.rearrange("p t (c i) -> p c t i", i=4),
-    )
 
 
 def quantise(nc, grouped, codes, scales):
@@ -43,18 +38,18 @@ def tile_gatedattentionunit_pb_kernel(tc, q, k, u, v, W_o, b_o, out):
 
         identity = const.tile([P, P], BF16)
         make_identity(nc, identity[:])
+        identity_words = const.tile([P, P], F32)
+        make_identity(nc, identity_words[:])
 
-        k_rows, q_rows, v_rows, u_rows = [], [], [], []
-        k_flipped, q_flipped, u_flipped = [], [], []
+        kq_rows, v_rows, u_rows = [], [], []
+        kq_flipped, u_flipped = [], []
         attn_mx, v_mx, gated_mx = [], [], []
         for b in range(B):
-            k_sb = batch.tile([P, PACK, S], BF16)
-            q_sb = batch.tile([P, CHUNKS, S], BF16)
+            kq_sb = batch.tile([P, 2, PACK, S], BF16)
             v_sb = batch.tile([P, PACK, H], BF16)
             u_sb = batch.tile([P, CHUNKS, H], BF16)
-            kT = batch.tile([P, PACK, P], BF16)
-            qT = batch.tile([P, CHUNKS, P], BF16)
-            uT = batch.tile([P, PASSES, CHUNKS, PACK, P], BF16)
+            kqT = batch.tile([P, 2, PACK, P], BF16)
+            uT = batch.tile([P, CHUNKS, H // SPAN, P], F32)
             attn_grouped = batch.tile([P, CHUNKS, P, PACK], BF16, align_bytes=64)
             attn_codes = batch.tile([P, N], U32, align_bytes=64)
             attn_scales = batch.tile([P, N], U8, align_bytes=64)
@@ -64,12 +59,10 @@ def tile_gatedattentionunit_pb_kernel(tc, q, k, u, v, W_o, b_o, out):
             gated_grouped = batch.tile([P, PASSES, CHUNKS, P, PACK], BF16, align_bytes=64)
             gated_codes = batch.tile([P, PASSES, N], U32, align_bytes=64)
             gated_scales = batch.tile([P, PASSES, N], U8, align_bytes=64)
-            k_rows.append(k_sb)
-            q_rows.append(q_sb)
+            kq_rows.append(kq_sb)
             v_rows.append(v_sb)
             u_rows.append(u_sb)
-            k_flipped.append(kT)
-            q_flipped.append(qT)
+            kq_flipped.append(kqT)
             u_flipped.append(uT)
             attn_mx.append((attn_grouped, attn_codes, attn_scales))
             v_mx.append((v_grouped, v_codes, v_scales))
@@ -80,106 +73,123 @@ def tile_gatedattentionunit_pb_kernel(tc, q, k, u, v, W_o, b_o, out):
         w_scales = const.tile([P, PASSES, D], U8, align_bytes=64)
         bias = const.tile([P, D], BF16)
 
-        def load_small(b):
-            nc.sync.dma_start(out=k_rows[b][:], in_=k[b].rearrange("(p t) s -> p t s", t=PACK))
-            nc.sync.dma_start(out=q_rows[b][:], in_=q[b].rearrange("(p c) s -> p c s", c=CHUNKS))
+        def load_keys_and_queries(b):
+            nc.sync.dma_start(out=kq_rows[b][:, 0], in_=k[b].rearrange("(p t) s -> p t s", t=PACK))
+            nc.sync.dma_start(out=kq_rows[b][:, 1], in_=q[b].rearrange("(p c) s -> p c s", c=CHUNKS))
 
-        def load_wide(rows_sb, rows):
+        def load_values(b):
             for half in halves:
                 nc.sync.dma_start(
-                    out=rows_sb[:, :, half], in_=rows.rearrange("(p i) h -> p i h", i=PACK)[:, :, half]
+                    out=v_rows[b][:, :, half], in_=v[b].rearrange("(p t) h -> p t h", t=PACK)[:, :, half]
                 )
 
-        load_small(0)
-        load_wide(v_rows[0], v[0])
-        load_wide(v_rows[1], v[1])
-        load_wide(u_rows[0], u[0])
-        load_small(1)
-        load_wide(u_rows[1], u[1])
+        def load_gate(b):
+            for chunks in (slice(0, CHUNKS // 2), slice(CHUNKS // 2, CHUNKS)):
+                nc.sync.dma_start(
+                    out=u_rows[b][:, chunks, :],
+                    in_=u[b].rearrange("(p c) h -> p c h", c=CHUNKS)[:, chunks, :],
+                )
+
+        load_keys_and_queries(0)
+        load_values(0)
+        load_keys_and_queries(1)
+        load_values(1)
+        load_gate(0)
+        load_gate(1)
         for g in range(PASSES):
             nc.sync.dma_start(
-                out=w_sb[:, g], in_=W_o[halves[g], :].rearrange("(t p) d -> p t d", t=PACK)
+                out=w_sb[:, g].rearrange("p (j e) d -> p j (e d)", e=PAIR),
+                in_=W_o[halves[g], :].rearrange("(j p e) d -> p j (e d)", p=P, e=PAIR),
             )
         nc.sync.dma_start(out=bias[:], in_=b_o.partition_broadcast(P))
 
-        def transpose_four(blocks, flipped_sb):
-            flipped = psum.tile([P, PACK, P], BF16, tag="plain")
-            for i in range(PACK):
-                nc.tensor.transpose(flipped[:, i, :], blocks[i], identity[:])
-            nc.scalar.copy(out=flipped_sb, in_=flipped[:])
-
         def transpose_keys_and_queries(b):
-            transpose_four([k_rows[b][:, t, :] for t in range(PACK)], k_flipped[b][:])
-            transpose_four([q_rows[b][:, c, :] for c in range(CHUNKS)], q_flipped[b][:])
-
-        def attention_weights(b):
-            for c in range(CHUNKS):
-                scores = psum.tile([P, PACK, P], F32, tag="plain")
+            flipped = psum.tile([P, 2, PACK, P], BF16, tag="plain")
+            for i in range(2):
                 for t in range(PACK):
-                    nc.tensor.matmul(
-                        out=scores[:, t, :],
-                        lhsT=k_flipped[b][:, t, :],
-                        rhs=q_flipped[b][:, c, :],
-                        start=True,
-                        stop=True,
-                    )
-                positive = work.tile([P, P, PACK], F32)
-                nc.scalar.activation(
-                    out=positive[:],
-                    in_=scores[:].rearrange("p t n -> p n t"),
-                    func=ACT.Relu,
-                    scale=1.0 / math.sqrt(S),
-                )
-                nc.scalar.activation(out=attn_mx[b][0][:, c], in_=positive[:], func=ACT.Square)
+                    nc.tensor.transpose(flipped[:, i, t, :], kq_rows[b][:, i, t, :], identity[:])
+            nc.scalar.copy(out=kq_flipped[b][:], in_=flipped[:])
 
-        def quantise_attention_weights(b):
+        def attention_chunk(b, c):
+            scores = psum.tile([P, PACK, P], F32, tag="plain")
+            for t in range(PACK):
+                nc.tensor.matmul(
+                    out=scores[:, t, :],
+                    lhsT=kq_flipped[b][:, 0, t, :],
+                    rhs=kq_flipped[b][:, 1, c, :],
+                    start=True,
+                    stop=True,
+                )
+            positive = work.tile([P, P, PACK], F32)
+            nc.scalar.activation(
+                out=positive[:],
+                in_=scores[:].rearrange("p t n -> p n t"),
+                func=ACT.Relu,
+                scale=1.0 / math.sqrt(S),
+            )
+            nc.scalar.activation(out=attn_mx[b][0][:, c], in_=positive[:], func=ACT.Square)
+
+        def quantise_attention_weights(b, first_chunk):
             grouped, codes, scales = attn_mx[b]
-            quantise(nc, grouped[:].rearrange("p c n t -> p (c n t)"), codes[:], scales[:])
+            chunks = slice(first_chunk, first_chunk + 2)
+            queries = slice(first_chunk * P, (first_chunk + 2) * P)
+            quantise(
+                nc, grouped[:, chunks].rearrange("p c n t -> p (c n t)"), codes[:, queries], scales[:, queries]
+            )
 
         def regroup_values(b):
-            for half in halves:
-                regroup(nc.vector.tensor_copy, v_mx[b][0][:, half, :], v_rows[b][:, :, half])
-
-        def quantise_values(b):
-            grouped, codes, scales = v_mx[b]
-            for half in halves:
-                quantise(
-                    nc, grouped[:, half, :].rearrange("p h t -> p (h t)"), codes[:, half], scales[:, half]
+            for first in range(0, H, SPAN):
+                span = slice(first, first + SPAN)
+                nc.vector.tensor_copy(
+                    out=v_mx[b][0][:, span, :].rearrange("p (e x i) t -> p x t i e", e=PAIR, i=2),
+                    in_=v_rows[b][:, :, span].rearrange("p t (x i e) -> p x t i e", e=PAIR, i=2),
                 )
+
+        def quantise_values(b, g):
+            grouped, codes, scales = v_mx[b]
+            half = halves[g]
+            quantise(nc, grouped[:, half, :].rearrange("p h t -> p (h t)"), codes[:, half], scales[:, half])
 
         def transpose_gate(b):
-            for g in range(PASSES):
-                for c in range(CHUNKS):
-                    hidden = [slice((g * PACK + t) * P, (g * PACK + t + 1) * P) for t in range(PACK)]
-                    transpose_four([u_rows[b][:, c, columns] for columns in hidden], u_flipped[b][:, g, c])
-
-        def gated_values(b, g):
-            grouped, codes, scales = gated_mx[b]
+            words = u_rows[b][:].bitcast(F32)
             for c in range(CHUNKS):
-                queries = slice(c * P, (c + 1) * P)
-                av = psum.tile([P, PACK, P], F32, tag="mx")
-                for t in range(PACK):
-                    hidden = slice((g * PACK + t) * P, (g * PACK + t + 1) * P)
-                    nc.tensor.matmul_mx(
-                        out=av[:, t, :],
-                        lhsT=v_mx[b][1][:, hidden].bitcast(FP8X4),
-                        lhsT_scale=v_mx[b][2][:, hidden],
-                        rhs=attn_mx[b][1][:, queries].bitcast(FP8X4),
-                        rhs_scale=attn_mx[b][2][:, queries],
-                        start=True,
-                        stop=True,
-                    )
-                nc.vector.tensor_tensor(
-                    out=grouped[:, g, c],
-                    in0=av[:].rearrange("p t n -> p n t"),
-                    in1=u_flipped[b][:, g, c].rearrange("p t n -> p n t"),
-                    op=ALU.mult,
+                flipped = psum.tile([P, H // SPAN, P], F32, tag="plain")
+                for i in range(H // SPAN):
+                    nc.tensor.transpose(flipped[:, i, :], words[:, c, i * P : (i + 1) * P], identity_words[:])
+                nc.scalar.copy(out=u_flipped[b][:, c], in_=flipped[:])
+
+        def gated_chunk(b, g, c):
+            queries = slice(c * P, (c + 1) * P)
+            av = psum.tile([P, PACK, P], F32, tag="mx")
+            for t in range(PACK):
+                hidden = slice((g * PACK + t) * P, (g * PACK + t + 1) * P)
+                nc.tensor.matmul_mx(
+                    out=av[:, t, :],
+                    lhsT=v_mx[b][1][:, hidden].bitcast(FP8X4),
+                    lhsT_scale=v_mx[b][2][:, hidden],
+                    rhs=attn_mx[b][1][:, queries].bitcast(FP8X4),
+                    rhs_scale=attn_mx[b][2][:, queries],
+                    start=True,
+                    stop=True,
                 )
+            gate = u_flipped[b][:].bitcast(BF16)[:, c, PAIR * g : PAIR * (g + 1), :]
+            nc.vector.tensor_tensor(
+                out=gated_mx[b][0][:, g, c].rearrange("p n (j e) -> p n j e", e=PAIR),
+                in0=av[:].rearrange("p (j e) n -> p n j e", e=PAIR),
+                in1=gate.rearrange("p j (n e) -> p n j e", e=PAIR),
+                op=ALU.mult,
+            )
+
+        def quantise_gated(b, g):
+            grouped, codes, scales = gated_mx[b]
             quantise(nc, grouped[:, g].rearrange("p c n t -> p (c n t)"), codes[:, g, :], scales[:, g, :])
 
         def regroup_weights():
             for g in range(PASSES):
-                regroup(nc.scalar.copy, w_grouped[:, g], w_sb[:, g])
+                nc.scalar.copy(
+                    out=w_grouped[:, g].rearrange("p (x i) t -> p x t i", i=4),
+                    in_=w_sb[:, g].rearrange("p t (x i) -> p x t i", i=4),
+                )
 
         def quantise_weights(g):
             quantise(nc, w_grouped[:, g].rearrange("p d t -> p (d t)"), w_codes[:, g, :], w_scales[:, g, :])
@@ -205,23 +215,36 @@ def tile_gatedattentionunit_pb_kernel(tc, q, k, u, v, W_o, b_o, out):
 
         with tc.manual_schedule():
             transpose_keys_and_queries(0)
-            attention_weights(0)
+            for c in range(CHUNKS):
+                attention_chunk(0, c)
             regroup_values(0)
-            quantise_values(0)
+            quantise_values(0, 0)
+            quantise_values(0, 1)
             regroup_values(1)
-            quantise_attention_weights(0)
-            quantise_values(1)
-            transpose_gate(0)
             transpose_keys_and_queries(1)
-            gated_values(0, 0)
-            attention_weights(1)
-            gated_values(0, 1)
-            quantise_attention_weights(1)
+            quantise_attention_weights(0, 0)
+            quantise_attention_weights(0, 2)
+            transpose_gate(0)
+            for c in range(CHUNKS):
+                gated_chunk(0, 0, c)
+            quantise_gated(0, 0)
+            for c in range(CHUNKS):
+                attention_chunk(1, c)
+                gated_chunk(0, 1, c)
+            quantise_gated(0, 1)
+            quantise_values(1, 0)
+            quantise_values(1, 1)
+            quantise_attention_weights(1, 0)
+            quantise_attention_weights(1, 2)
             transpose_gate(1)
             regroup_weights()
-            gated_values(1, 0)
+            for c in range(CHUNKS):
+                gated_chunk(1, 0, c)
+            quantise_gated(1, 0)
             quantise_weights(0)
-            gated_values(1, 1)
+            for c in range(CHUNKS):
+                gated_chunk(1, 1, c)
             quantise_weights(1)
+            quantise_gated(1, 1)
             project(0)
             project(1)

@@ -46,7 +46,8 @@ def tile_gatedattentionunit_pb_kernel(tc, q, k, u, v, W_o, b_o, out):
         attn_mx, v_mx, gated_mx = [], [], []
         for b in range(B):
             kq_sb = batch.tile([P, 2, PACK, S], BF16)
-            v_sb = batch.tile([P, PACK, H], BF16)
+            v_first = batch.tile([P, PACK, H // 2], BF16)
+            v_second = batch.tile([P, PACK, H // 2], BF16)
             u_sb = batch.tile([P, CHUNKS, H], BF16)
             kqT = batch.tile([P, 2, PACK, P], BF16)
             uT = batch.tile([P, CHUNKS, H // SPAN, P], F32)
@@ -60,7 +61,7 @@ def tile_gatedattentionunit_pb_kernel(tc, q, k, u, v, W_o, b_o, out):
             gated_codes = batch.tile([P, PASSES, N], U32, align_bytes=64)
             gated_scales = batch.tile([P, PASSES, N], U8, align_bytes=64)
             kq_rows.append(kq_sb)
-            v_rows.append(v_sb)
+            v_rows.append((v_first, v_second))
             u_rows.append(u_sb)
             kq_flipped.append(kqT)
             u_flipped.append(uT)
@@ -77,11 +78,10 @@ def tile_gatedattentionunit_pb_kernel(tc, q, k, u, v, W_o, b_o, out):
             nc.sync.dma_start(out=kq_rows[b][:, 0], in_=k[b].rearrange("(p t) s -> p t s", t=PACK))
             nc.sync.dma_start(out=kq_rows[b][:, 1], in_=q[b].rearrange("(p c) s -> p c s", c=CHUNKS))
 
-        def load_values(b):
-            for half in halves:
-                nc.sync.dma_start(
-                    out=v_rows[b][:, :, half], in_=v[b].rearrange("(p t) h -> p t h", t=PACK)[:, :, half]
-                )
+        def load_values(b, g):
+            nc.sync.dma_start(
+                out=v_rows[b][g][:], in_=v[b].rearrange("(p t) h -> p t h", t=PACK)[:, :, halves[g]]
+            )
 
         def load_gate(b):
             for chunks in (slice(0, CHUNKS // 2), slice(CHUNKS // 2, CHUNKS)):
@@ -91,9 +91,11 @@ def tile_gatedattentionunit_pb_kernel(tc, q, k, u, v, W_o, b_o, out):
                 )
 
         load_keys_and_queries(0)
-        load_values(0)
+        load_values(0, 0)
+        load_values(0, 1)
         load_keys_and_queries(1)
-        load_values(1)
+        load_values(1, 0)
+        load_values(1, 1)
         load_gate(0)
         load_gate(1)
         for g in range(PASSES):
@@ -138,12 +140,17 @@ def tile_gatedattentionunit_pb_kernel(tc, q, k, u, v, W_o, b_o, out):
             )
 
         def regroup_values(b):
-            for first in range(0, H, SPAN):
-                span = slice(first, first + SPAN)
-                nc.vector.tensor_copy(
-                    out=v_mx[b][0][:, span, :].rearrange("p (e x i) t -> p x t i e", e=PAIR, i=2),
-                    in_=v_rows[b][:, :, span].rearrange("p t (x i e) -> p x t i e", e=PAIR, i=2),
-                )
+            for g in range(PASSES):
+                for j in range(PAIR):
+                    first = g * (H // 2) + j * SPAN
+                    nc.vector.tensor_copy(
+                        out=v_mx[b][0][:, first : first + SPAN, :].rearrange(
+                            "p (e x i) t -> p x t i e", e=PAIR, i=2
+                        ),
+                        in_=v_rows[b][g][:, :, j * SPAN : (j + 1) * SPAN].rearrange(
+                            "p t (x i e) -> p x t i e", e=PAIR, i=2
+                        ),
+                    )
 
         def quantise_values(b, g):
             grouped, codes, scales = v_mx[b]
@@ -222,18 +229,18 @@ def tile_gatedattentionunit_pb_kernel(tc, q, k, u, v, W_o, b_o, out):
             quantise_values(0, 1)
             regroup_values(1)
             transpose_keys_and_queries(1)
+            quantise_values(1, 0)
+            quantise_values(1, 1)
             quantise_attention_weights(0, 0)
             quantise_attention_weights(0, 2)
             transpose_gate(0)
             for c in range(CHUNKS):
                 gated_chunk(0, 0, c)
+                attention_chunk(1, c)
             quantise_gated(0, 0)
             for c in range(CHUNKS):
-                attention_chunk(1, c)
                 gated_chunk(0, 1, c)
             quantise_gated(0, 1)
-            quantise_values(1, 0)
-            quantise_values(1, 1)
             quantise_attention_weights(1, 0)
             quantise_attention_weights(1, 2)
             transpose_gate(1)

@@ -44,6 +44,7 @@ def tile_gatedattentionunit_pb_kernel(tc, q, k, u, v, W_o, b_o, out):
         kq_rows, v_rows, u_rows = [], [], []
         kq_flipped, u_flipped = [], []
         attn_mx, v_mx, gated_mx = [], [], []
+        results = []
         for b in range(B):
             kq_sb = batch.tile([P, 2, PACK, S], BF16)
             v_first = batch.tile([P, PACK, H // 2], BF16)
@@ -60,6 +61,7 @@ def tile_gatedattentionunit_pb_kernel(tc, q, k, u, v, W_o, b_o, out):
             gated_grouped = batch.tile([P, PASSES, CHUNKS, P, PACK], BF16, align_bytes=64)
             gated_codes = batch.tile([P, PASSES, N], U32, align_bytes=64)
             gated_scales = batch.tile([P, PASSES, N], U8, align_bytes=64)
+            result = batch.tile([P, CHUNKS, D], F32)
             kq_rows.append(kq_sb)
             v_rows.append((v_first, v_second))
             u_rows.append(u_sb)
@@ -68,6 +70,7 @@ def tile_gatedattentionunit_pb_kernel(tc, q, k, u, v, W_o, b_o, out):
             attn_mx.append((attn_grouped, attn_codes, attn_scales))
             v_mx.append((v_grouped, v_codes, v_scales))
             gated_mx.append((gated_grouped, gated_codes, gated_scales))
+            results.append(result)
         w_sb = const.tile([P, PASSES, PACK, D], BF16)
         w_grouped = const.tile([P, PASSES, D, PACK], BF16, align_bytes=64)
         w_codes = const.tile([P, PASSES, D], U32, align_bytes=64)
@@ -112,7 +115,7 @@ def tile_gatedattentionunit_pb_kernel(tc, q, k, u, v, W_o, b_o, out):
                     nc.tensor.transpose(flipped[:, i, t, :], kq_rows[b][:, i, t, :], identity[:])
             nc.scalar.copy(out=kq_flipped[b][:], in_=flipped[:])
 
-        def attention_chunk(b, c):
+        def positive_scores(b, c):
             scores = psum.tile([P, PACK, P], F32, tag="plain")
             for t in range(PACK):
                 nc.tensor.matmul(
@@ -129,7 +132,20 @@ def tile_gatedattentionunit_pb_kernel(tc, q, k, u, v, W_o, b_o, out):
                 func=ACT.Relu,
                 scale=1.0 / math.sqrt(S),
             )
+            return positive
+
+        def square(b, c, positive):
             nc.scalar.activation(out=attn_mx[b][0][:, c], in_=positive[:], func=ACT.Square)
+
+        def attention_weights(b, meanwhile):
+            waiting = None
+            for c in range(CHUNKS):
+                meanwhile(c)
+                positive = positive_scores(b, c)
+                if c > 0:
+                    square(b, c - 1, waiting)
+                waiting = positive
+            square(b, CHUNKS - 1, waiting)
 
         def quantise_attention_weights(b, first_chunk):
             grouped, codes, scales = attn_mx[b]
@@ -201,29 +217,30 @@ def tile_gatedattentionunit_pb_kernel(tc, q, k, u, v, W_o, b_o, out):
         def quantise_weights(g):
             quantise(nc, w_grouped[:, g].rearrange("p d t -> p (d t)"), w_codes[:, g, :], w_scales[:, g, :])
 
-        def project(b):
-            out_chunks = out[b].rearrange("(p c) d -> p c d", c=CHUNKS)
-            result = batch.tile([P, CHUNKS, D], F32)
-            for c in range(CHUNKS):
-                queries = slice(c * P, (c + 1) * P)
-                acc = psum.tile([P, D], F32, tag="mx")
-                for g in range(PASSES):
-                    nc.tensor.matmul_mx(
-                        out=acc[:],
-                        lhsT=gated_mx[b][1][:, g, queries].bitcast(FP8X4),
-                        lhsT_scale=gated_mx[b][2][:, g, queries],
-                        rhs=w_codes[:, g, :].bitcast(FP8X4),
-                        rhs_scale=w_scales[:, g, :],
-                        start=(g == 0),
-                        stop=(g == PASSES - 1),
-                    )
-                nc.vector.tensor_tensor(out=result[:, c, :], in0=acc[:], in1=bias[:], op=ALU.add)
-                nc.sync.dma_start(out=out_chunks[:, c, :], in_=result[:, c, :])
+        def project_chunk(b, c, tag):
+            queries = slice(c * P, (c + 1) * P)
+            acc = psum.tile([P, D], F32, tag=tag)
+            for g in range(PASSES):
+                nc.tensor.matmul_mx(
+                    out=acc[:],
+                    lhsT=gated_mx[b][1][:, g, queries].bitcast(FP8X4),
+                    lhsT_scale=gated_mx[b][2][:, g, queries],
+                    rhs=w_codes[:, g, :].bitcast(FP8X4),
+                    rhs_scale=w_scales[:, g, :],
+                    start=(g == 0),
+                    stop=(g == PASSES - 1),
+                )
+            return acc
+
+        def add_bias_and_store(b, c, acc):
+            nc.vector.tensor_tensor(out=results[b][:, c, :], in0=acc[:], in1=bias[:], op=ALU.add)
+            nc.sync.dma_start(
+                out=out[b].rearrange("(p c) d -> p c d", c=CHUNKS)[:, c, :], in_=results[b][:, c, :]
+            )
 
         with tc.manual_schedule():
             transpose_keys_and_queries(0)
-            for c in range(CHUNKS):
-                attention_chunk(0, c)
+            attention_weights(0, lambda c: None)
             regroup_values(0)
             quantise_values(0, 0)
             quantise_values(0, 1)
@@ -234,24 +251,29 @@ def tile_gatedattentionunit_pb_kernel(tc, q, k, u, v, W_o, b_o, out):
             quantise_attention_weights(0, 0)
             quantise_attention_weights(0, 2)
             transpose_gate(0)
-            for c in range(CHUNKS):
-                gated_chunk(0, 0, c)
-                attention_chunk(1, c)
+            attention_weights(1, lambda c: gated_chunk(0, 0, c))
+            gated_chunk(0, 1, 0)
             quantise_gated(0, 0)
-            for c in range(CHUNKS):
+            for c in range(1, CHUNKS):
                 gated_chunk(0, 1, c)
-            quantise_gated(0, 1)
             quantise_attention_weights(1, 0)
+            quantise_gated(0, 1)
             quantise_attention_weights(1, 2)
             transpose_gate(1)
             regroup_weights()
             for c in range(CHUNKS):
                 gated_chunk(1, 0, c)
+            gated_chunk(1, 1, 0)
             quantise_gated(1, 0)
             quantise_weights(0)
-            for c in range(CHUNKS):
-                gated_chunk(1, 1, c)
+            gated_chunk(1, 1, 1)
             quantise_weights(1)
+            for c in range(2, CHUNKS):
+                gated_chunk(1, 1, c)
+            projected = [project_chunk(0, c, "plain") for c in range(CHUNKS)]
+            add_bias_and_store(0, 0, projected[0])
             quantise_gated(1, 1)
-            project(0)
-            project(1)
+            for c in range(1, CHUNKS):
+                add_bias_and_store(0, c, projected[c])
+            for c in range(CHUNKS):
+                add_bias_and_store(1, c, project_chunk(1, c, "mx"))

@@ -108,12 +108,12 @@ def tile_gatedattentionunit_pb_kernel(tc, q, k, u, v, W_o, b_o, out):
             )
         nc.sync.dma_start(out=bias[:], in_=b_o.partition_broadcast(P))
 
-        def transpose_keys_and_queries(b):
+        def transpose_keys_and_queries(b, copy):
             flipped = psum.tile([P, 2, PACK, P], BF16, tag="plain")
             for i in range(2):
                 for t in range(PACK):
                     nc.tensor.transpose(flipped[:, i, t, :], kq_rows[b][:, i, t, :], identity[:])
-            nc.scalar.copy(out=kq_flipped[b][:], in_=flipped[:])
+            copy(out=kq_flipped[b][:], in_=flipped[:])
 
         def positive_scores(b, c):
             scores = psum.tile([P, PACK, P], F32, tag="plain")
@@ -239,16 +239,16 @@ def tile_gatedattentionunit_pb_kernel(tc, q, k, u, v, W_o, b_o, out):
             )
 
         with tc.manual_schedule():
-            transpose_keys_and_queries(0)
+            transpose_keys_and_queries(0, nc.scalar.copy)
             attention_weights(0, lambda c: None)
             regroup_values(0)
             quantise_values(0, 0)
             quantise_values(0, 1)
             regroup_values(1)
-            transpose_keys_and_queries(1)
+            transpose_keys_and_queries(1, nc.vector.tensor_copy)
             quantise_values(1, 0)
-            quantise_values(1, 1)
             quantise_attention_weights(0, 0)
+            quantise_values(1, 1)
             quantise_attention_weights(0, 2)
             transpose_gate(0)
             attention_weights(1, lambda c: gated_chunk(0, 0, c))

@@ -108,12 +108,12 @@ def tile_gatedattentionunit_pb_kernel(tc, q, k, u, v, W_o, b_o, out):
             )
         nc.sync.dma_start(out=bias[:], in_=b_o.partition_broadcast(P))
 
-        def transpose_keys_and_queries(b, copy):
+        def transpose_keys_and_queries(b):
             flipped = psum.tile([P, 2, PACK, P], BF16, tag="plain")
             for i in range(2):
                 for t in range(PACK):
                     nc.tensor.transpose(flipped[:, i, t, :], kq_rows[b][:, i, t, :], identity[:])
-            copy(out=kq_flipped[b][:], in_=flipped[:])
+            nc.scalar.copy(out=kq_flipped[b][:], in_=flipped[:])
 
         def positive_scores(b, c):
             scores = psum.tile([P, PACK, P], F32, tag="plain")
@@ -217,20 +217,17 @@ def tile_gatedattentionunit_pb_kernel(tc, q, k, u, v, W_o, b_o, out):
         def quantise_weights(g):
             quantise(nc, w_grouped[:, g].rearrange("p d t -> p (d t)"), w_codes[:, g, :], w_scales[:, g, :])
 
-        def project_chunk(b, c, tag):
+        def project_pass(b, c, g, acc):
             queries = slice(c * P, (c + 1) * P)
-            acc = psum.tile([P, D], F32, tag=tag)
-            for g in range(PASSES):
-                nc.tensor.matmul_mx(
-                    out=acc[:],
-                    lhsT=gated_mx[b][1][:, g, queries].bitcast(FP8X4),
-                    lhsT_scale=gated_mx[b][2][:, g, queries],
-                    rhs=w_codes[:, g, :].bitcast(FP8X4),
-                    rhs_scale=w_scales[:, g, :],
-                    start=(g == 0),
-                    stop=(g == PASSES - 1),
-                )
-            return acc
+            nc.tensor.matmul_mx(
+                out=acc[:],
+                lhsT=gated_mx[b][1][:, g, queries].bitcast(FP8X4),
+                lhsT_scale=gated_mx[b][2][:, g, queries],
+                rhs=w_codes[:, g, :].bitcast(FP8X4),
+                rhs_scale=w_scales[:, g, :],
+                start=(g == 0),
+                stop=(g == PASSES - 1),
+            )
 
         def add_bias_and_store(b, c, acc):
             nc.vector.tensor_tensor(out=results[b][:, c, :], in0=acc[:], in1=bias[:], op=ALU.add)
@@ -239,16 +236,16 @@ def tile_gatedattentionunit_pb_kernel(tc, q, k, u, v, W_o, b_o, out):
             )
 
         with tc.manual_schedule():
-            transpose_keys_and_queries(0, nc.scalar.copy)
+            transpose_keys_and_queries(0)
             attention_weights(0, lambda c: None)
             regroup_values(0)
             quantise_values(0, 0)
             quantise_values(0, 1)
             regroup_values(1)
-            transpose_keys_and_queries(1, nc.vector.tensor_copy)
+            transpose_keys_and_queries(1)
             quantise_values(1, 0)
-            quantise_attention_weights(0, 0)
             quantise_values(1, 1)
+            quantise_attention_weights(0, 0)
             quantise_attention_weights(0, 2)
             transpose_gate(0)
             attention_weights(1, lambda c: gated_chunk(0, 0, c))
@@ -266,14 +263,16 @@ def tile_gatedattentionunit_pb_kernel(tc, q, k, u, v, W_o, b_o, out):
             gated_chunk(1, 1, 0)
             quantise_gated(1, 0)
             quantise_weights(0)
-            gated_chunk(1, 1, 1)
-            quantise_weights(1)
-            for c in range(2, CHUNKS):
-                gated_chunk(1, 1, c)
-            projected = [project_chunk(0, c, "plain") for c in range(CHUNKS)]
-            add_bias_and_store(0, 0, projected[0])
-            quantise_gated(1, 1)
             for c in range(1, CHUNKS):
-                add_bias_and_store(0, c, projected[c])
-            for c in range(CHUNKS):
-                add_bias_and_store(1, c, project_chunk(1, c, "mx"))
+                gated_chunk(1, 1, c)
+            quantise_weights(1)
+            quantise_gated(1, 1)
+            banks = ("plain", "mx")
+            sums = [[psum.tile([P, D], F32, tag=banks[b], name="acc") for c in range(CHUNKS)] for b in range(B)]
+            for g in range(PASSES):
+                for b in range(B):
+                    for c in range(CHUNKS):
+                        project_pass(b, c, g, sums[b][c])
+            for b in range(B):
+                for c in range(CHUNKS):
+                    add_bias_and_store(b, c, sums[b][c])

import math
from contextlib import ExitStack

import concourse.mybir as mybir
from concourse.masks import make_identity

BF16 = mybir.dt.bfloat16
F32 = mybir.dt.float32
U32 = mybir.dt.uint32
U8 = mybir.dt.uint8
FP8X4 = mybir.dt.float8_e4m3fn_x4
ACT = mybir.ActivationFunctionType
ALU = mybir.AluOpType

P = 128
PACK = 4
PAIR = 2
B, N, S, H, D = 2, 512, 128, 1024, 512
CHUNKS = N // P
PASSES = H // (P * PACK)
SPAN = P * PAIR

FLOPS = 2 * B * N * N * S + 2 * B * N * N * H + 2 * B * N * H * D


def quantise(nc, grouped, codes, scales):
    nc.vector.quantize_mx(out=codes.bitcast(FP8X4), scales=scales, in_=grouped)


def tile_gatedattentionunit_pb_kernel(tc, q, k, u, v, W_o, b_o, out):
    nc = tc.nc
    halves = [slice(g * (H // 2), (g + 1) * (H // 2)) for g in range(PASSES)]
    with ExitStack() as ctx:
        const = ctx.enter_context(tc.tile_pool(name="const", bufs=1))
        batch = ctx.enter_context(tc.tile_pool(name="batch", bufs=B))
        work = ctx.enter_context(tc.tile_pool(name="work", bufs=2))
        psum = ctx.enter_context(tc.psum_pool(name="psum", bufs=4))

        identity = const.tile([P, P], BF16)
        make_identity(nc, identity[:])
        identity_words = const.tile([P, P], F32)
        make_identity(nc, identity_words[:])

        kq_rows, v_rows, u_rows = [], [], []
        kq_flipped, u_flipped = [], []
        attn_mx, v_mx, gated_mx = [], [], []
        results = []
        for b in range(B):
            kq_sb = batch.tile([P, 2, PACK, S], BF16)
            v_first = batch.tile([P, PACK, H // 2], BF16)
            v_second = batch.tile([P, PACK, H // 2], BF16)
            u_sb = batch.tile([P, CHUNKS, H], BF16)
            kqT = batch.tile([P, 2, PACK, P], BF16)
            uT = batch.tile([P, CHUNKS, H // SPAN, P], F32)
            attn_grouped = batch.tile([P, CHUNKS, P, PACK], BF16, align_bytes=64)
            attn_codes = batch.tile([P, N], U32, align_bytes=64)
            attn_scales = batch.tile([P, N], U8, align_bytes=64)
            v_grouped = batch.tile([P, H, PACK], BF16, align_bytes=64)
            v_codes = batch.tile([P, H], U32, align_bytes=64)
            v_scales = batch.tile([P, H], U8, align_bytes=64)
            gated_grouped = batch.tile([P, PASSES, CHUNKS, P, PACK], BF16, align_bytes=64)
            gated_codes = batch.tile([P, PASSES, N], U32, align_bytes=64)
            gated_scales = batch.tile([P, PASSES, N], U8, align_bytes=64)
            result = batch.tile([P, CHUNKS, D], F32)
            kq_rows.append(kq_sb)
            v_rows.append((v_first, v_second))
            u_rows.append(u_sb)
            kq_flipped.append(kqT)
            u_flipped.append(uT)
            attn_mx.append((attn_grouped, attn_codes, attn_scales))
            v_mx.append((v_grouped, v_codes, v_scales))
            gated_mx.append((gated_grouped, gated_codes, gated_scales))
            results.append(result)
        w_sb = const.tile([P, PASSES, PACK, D], BF16)
        w_grouped = const.tile([P, PASSES, D, PACK], BF16, align_bytes=64)
        w_codes = const.tile([P, PASSES, D], U32, align_bytes=64)
        w_scales = const.tile([P, PASSES, D], U8, align_bytes=64)
        bias = const.tile([P, D], BF16)

        def load_keys_and_queries(b):
            nc.sync.dma_start(out=kq_rows[b][:, 0], in_=k[b].rearrange("(p t) s -> p t s", t=PACK))
            nc.sync.dma_start(out=kq_rows[b][:, 1], in_=q[b].rearrange("(p c) s -> p c s", c=CHUNKS))

        def load_values(b, g):
            nc.sync.dma_start(
                out=v_rows[b][g][:], in_=v[b].rearrange("(p t) h -> p t h", t=PACK)[:, :, halves[g]]
            )

        def load_gate(b):
            for chunks in (slice(0, CHUNKS // 2), slice(CHUNKS // 2, CHUNKS)):
                nc.sync.dma_start(
                    out=u_rows[b][:, chunks, :],
                    in_=u[b].rearrange("(p c) h -> p c h", c=CHUNKS)[:, chunks, :],
                )

        load_keys_and_queries(0)
        load_values(0, 0)
        load_values(0, 1)
        load_keys_and_queries(1)
        load_values(1, 0)
        load_values(1, 1)
        load_gate(0)
        load_gate(1)
        for g in range(PASSES):
            nc.sync.dma_start(
                out=w_sb[:, g].rearrange("p (j e) d -> p j (e d)", e=PAIR),
                in_=W_o[halves[g], :].rearrange("(j p e) d -> p j (e d)", p=P, e=PAIR),
            )
        nc.sync.dma_start(out=bias[:], in_=b_o.partition_broadcast(P))

        def transpose_keys_and_queries(b):
            flipped = psum.tile([P, 2, PACK, P], BF16, tag="plain")
            for i in range(2):
                for t in range(PACK):
                    nc.tensor.transpose(flipped[:, i, t, :], kq_rows[b][:, i, t, :], identity[:])
            nc.scalar.copy(out=kq_flipped[b][:], in_=flipped[:])

        def positive_scores(b, c):
            scores = psum.tile([P, PACK, P], F32, tag="plain")
            for t in range(PACK):
                nc.tensor.matmul(
                    out=scores[:, t, :],
                    lhsT=kq_flipped[b][:, 0, t, :],
                    rhs=kq_flipped[b][:, 1, c, :],
                    start=True,
                    stop=True,
                )
            positive = work.tile([P, P, PACK], F32)
            nc.scalar.activation(
                out=positive[:],
                in_=scores[:].rearrange("p t n -> p n t"),
                func=ACT.Relu,
                scale=1.0 / math.sqrt(S),
            )
            return positive

        def square(b, c, positive):
            nc.scalar.activation(out=attn_mx[b][0][:, c], in_=positive[:], func=ACT.Square)

        def attention_weights(b, meanwhile):
            waiting = None
            for c in range(CHUNKS):
                meanwhile(c)
                positive = positive_scores(b, c)
                if c > 0:
                    square(b, c - 1, waiting)
                waiting = positive
            square(b, CHUNKS - 1, waiting)

        def quantise_attention_weights(b, first_chunk):
            grouped, codes, scales = attn_mx[b]
            chunks = slice(first_chunk, first_chunk + 2)
            queries = slice(first_chunk * P, (first_chunk + 2) * P)
            quantise(
                nc, grouped[:, chunks].rearrange("p c n t -> p (c n t)"), codes[:, queries], scales[:, queries]
            )

        def regroup_values(b):
            for g in range(PASSES):
                for j in range(PAIR):
                    first = g * (H // 2) + j * SPAN
                    nc.vector.tensor_copy(
                        out=v_mx[b][0][:, first : first + SPAN, :].rearrange(
                            "p (e x i) t -> p x t i e", e=PAIR, i=2
                        ),
                        in_=v_rows[b][g][:, :, j * SPAN : (j + 1) * SPAN].rearrange(
                            "p t (x i e) -> p x t i e", e=PAIR, i=2
                        ),
                    )

        def quantise_values(b, g):
            grouped, codes, scales = v_mx[b]
            half = halves[g]
            quantise(nc, grouped[:, half, :].rearrange("p h t -> p (h t)"), codes[:, half], scales[:, half])

        def transpose_gate(b):
            words = u_rows[b][:].bitcast(F32)
            for c in range(CHUNKS):
                flipped = psum.tile([P, H // SPAN, P], F32, tag="plain")
                for i in range(H // SPAN):
                    nc.tensor.transpose(flipped[:, i, :], words[:, c, i * P : (i + 1) * P], identity_words[:])
                nc.scalar.copy(out=u_flipped[b][:, c], in_=flipped[:])

        def gated_chunk(b, g, c):
            queries = slice(c * P, (c + 1) * P)
            av = psum.tile([P, PACK, P], F32, tag="mx")
            for t in range(PACK):
                hidden = slice((g * PACK + t) * P, (g * PACK + t + 1) * P)
                nc.tensor.matmul_mx(
                    out=av[:, t, :],
                    lhsT=v_mx[b][1][:, hidden].bitcast(FP8X4),
                    lhsT_scale=v_mx[b][2][:, hidden],
                    rhs=attn_mx[b][1][:, queries].bitcast(FP8X4),
                    rhs_scale=attn_mx[b][2][:, queries],
                    start=True,
                    stop=True,
                )
            gate = u_flipped[b][:].bitcast(BF16)[:, c, PAIR * g : PAIR * (g + 1), :]
            nc.vector.tensor_tensor(
                out=gated_mx[b][0][:, g, c].rearrange("p n (j e) -> p n j e", e=PAIR),
                in0=av[:].rearrange("p (j e) n -> p n j e", e=PAIR),
                in1=gate.rearrange("p j (n e) -> p n j e", e=PAIR),
                op=ALU.mult,
            )

        def quantise_gated(b, g):
            grouped, codes, scales = gated_mx[b]
            quantise(nc, grouped[:, g].rearrange("p c n t -> p (c n t)"), codes[:, g, :], scales[:, g, :])

        def regroup_weights():
            for g in range(PASSES):
                nc.scalar.copy(
                    out=w_grouped[:, g].rearrange("p (x i) t -> p x t i", i=4),
                    in_=w_sb[:, g].rearrange("p t (x i) -> p x t i", i=4),
                )

        def quantise_weights(g):
            quantise(nc, w_grouped[:, g].rearrange("p d t -> p (d t)"), w_codes[:, g, :], w_scales[:, g, :])

        def project_pass(b, c, g, acc):
            queries = slice(c * P, (c + 1) * P)
            nc.tensor.matmul_mx(
                out=acc[:],
                lhsT=gated_mx[b][1][:, g, queries].bitcast(FP8X4),
                lhsT_scale=gated_mx[b][2][:, g, queries],
                rhs=w_codes[:, g, :].bitcast(FP8X4),
                rhs_scale=w_scales[:, g, :],
                start=(g == 0),
                stop=(g == PASSES - 1),
            )

        def add_bias_and_store(b, c, acc):
            nc.vector.tensor_tensor(out=results[b][:, c, :], in0=acc[:], in1=bias[:], op=ALU.add)
            nc.sync.dma_start(
                out=out[b].rearrange("(p c) d -> p c d", c=CHUNKS)[:, c, :], in_=results[b][:, c, :]
            )

        with tc.manual_schedule():
            transpose_keys_and_queries(0)
            attention_weights(0, lambda c: None)
            regroup_values(0)
            quantise_values(0, 0)
            quantise_values(0, 1)
            regroup_values(1)
            transpose_keys_and_queries(1)
            quantise_values(1, 0)
            quantise_values(1, 1)
            quantise_attention_weights(0, 0)
            quantise_attention_weights(0, 2)
            transpose_gate(0)
            attention_weights(1, lambda c: gated_chunk(0, 0, c))
            gated_chunk(0, 1, 0)
            quantise_gated(0, 0)
            for c in range(1, CHUNKS):
                gated_chunk(0, 1, c)
            quantise_attention_weights(1, 0)
            quantise_gated(0, 1)
            quantise_attention_weights(1, 2)
            transpose_gate(1)
            regroup_weights()
            for c in range(CHUNKS):
                gated_chunk(1, 0, c)
            gated_chunk(1, 1, 0)
            quantise_gated(1, 0)
            quantise_weights(0)
            for c in range(1, CHUNKS):
                gated_chunk(1, 1, c)
            quantise_weights(1)
            quantise_gated(1, 1)
            banks = ("plain", "mx")
            sums = [[psum.tile([P, D], F32, tag=banks[b], name="acc") for c in range(CHUNKS)] for b in range(B)]
            for g in range(PASSES):
                for b in range(B):
                    for c in range(CHUNKS):
                        project_pass(b, c, g, sums[b][c])
            for b in range(B):
                for c in range(CHUNKS):
                    add_bias_and_store(b, c, sums[b][c])
